import numpy as np
import ml_dtypes


def mxq(x, axis, fmt="e4m3"):
    dtype, down = {"e4m3": (ml_dtypes.float8_e4m3fn, 7), "e5m2": (ml_dtypes.float8_e5m2, 14)}[fmt]
    v = np.moveaxis(np.asarray(x, np.float32).astype(ml_dtypes.bfloat16).astype(np.float64), axis, -1)
    blocks = v.reshape(v.shape[:-1] + (-1, 32))
    amax = np.abs(blocks).max(-1, keepdims=True)
    byte = np.maximum(np.where(amax > 0, np.frexp(amax)[1] - 1 + 127, 0) - down, 1)
    scale = np.exp2(byte - 127.0)
    codes = (blocks / scale).astype(np.float32).astype(dtype).astype(np.float64)
    return np.moveaxis((codes * scale).reshape(v.shape), -1, axis)


WIDE = False


def mx_kscale(k):
    if not WIDE:
        return np.ones(k)
    levels = np.array([10, -10, 5, -5, 0])
    a = np.random.permutation(np.resize(levels, k // 512 * 4)).reshape(k // 512, 4)
    idx = np.arange(k)
    return np.exp2(a[idx // 512, idx % 128 // 32])


BF16 = ml_dtypes.bfloat16


def bf(x):
    return np.asarray(x, np.float32).astype(BF16)


def f64(x):
    return np.asarray(x).astype(np.float64)


B, S, HID, H, KV, D, T = 4, 2048, 1024, 2, 1, 64, 2048
DQ = H * D
DKV = KV * D
OUT = DQ + 2 * DKV
THETA = 1e4


def make_pos_emb():
    i = np.repeat(np.arange(D // 2), 2)
    freq = np.power(THETA, -i * 2.0 / D)
    t = freq[:, None] * f64(np.arange(T))[None, :]
    cos = np.cos(t)
    sin = np.sin(t)
    sin[0::2] *= -1.0
    return np.concatenate([cos, sin], axis=0).T


def flip_pairs(x):
    return x.reshape(x.shape[:-1] + (D // 2, 2))[..., ::-1].reshape(x.shape)


def apply_rope(x, pe):
    return x * pe[:, :D] + flip_pairs(x) * pe[:, D:]


def setup_inputs():
    s = mx_kscale(HID)
    return {"tensor": bf(np.random.standard_normal((B, S, HID)) * s),
            "w_qkv": bf(np.random.standard_normal((OUT, HID)) * 1.5 / np.sqrt(HID) / s[None, :]),
            "b_qkv": bf(np.random.standard_normal(OUT) * 0.3),
            "pos_emb": bf(make_pos_emb())}


def reference(tensor, w_qkv, b_qkv, pos_emb):
    qkv = (mxq(f64(tensor), 2, "e4m3") @ mxq(f64(w_qkv), 1, "e4m3").T) + f64(b_qkv)
    q = qkv[..., :DQ].reshape(B, S, H, D).transpose(0, 2, 1, 3)
    k = qkv[..., DQ:DQ + DKV].reshape(B, S, KV, D).transpose(0, 2, 1, 3)
    v = qkv[..., DQ + DKV:].reshape(B, S, KV, D).transpose(0, 2, 1, 3)
    pe = f64(pos_emb)[:S]
    return apply_rope(q, pe), apply_rope(k, pe), v

@@ -1,0 +1,213 @@
+from contextlib import ExitStack
+
+import concourse.mybir as mybir
+from concourse.masks import make_identity
+
+FLOPS = 2 * 8192 * 1024 * 256
+
+F32 = mybir.dt.float32
+BF16 = mybir.dt.bfloat16
+U32 = mybir.dt.uint32
+U8 = mybir.dt.uint8
+FP8X4 = mybir.dt.float8_e4m3fn_x4
+ADD = mybir.AluOpType.add
+MULT = mybir.AluOpType.mult
+
+P = 128
+NB = 4
+TPP = 16
+HID = 1024
+RT = 4
+ROUNDS = NB * TPP // RT
+
+MANUAL = True
+A2_GPSIMD = True
+V_OFF_VECTOR = False
+
+
+def tile_multiqueryattention_pa_t_kernel(tc, tensor, w_qkv, b_qkv, pos_emb, out_0, out_1, out_2):
+    nc = tc.nc
+    with ExitStack() as ctx:
+        const = ctx.enter_context(tc.tile_pool(name="const", bufs=1))
+        xpool = ctx.enter_context(tc.tile_pool(name="xpool", bufs=1))
+        gpool = ctx.enter_context(tc.tile_pool(name="gpool", bufs=2))
+        cpool = ctx.enter_context(tc.tile_pool(name="cpool", bufs=2))
+        mpool = ctx.enter_context(tc.tile_pool(name="mpool", bufs=4))
+        ypool = ctx.enter_context(tc.tile_pool(name="ypool", bufs=3))
+        psum = ctx.enter_context(tc.psum_pool(name="psum", bufs=1))
+        if MANUAL:
+            ctx.enter_context(tc.manual_schedule())
+
+        bb = const.tile([P, 256], BF16, name="bb")
+        nc.scalar.dma_start(out=bb[:], in_=b_qkv.partition_broadcast(P))
+        w_sb = const.tile([P, 2, HID], BF16, name="w_sb")
+        nc.sync.dma_start(out=w_sb[:], in_=w_qkv.rearrange("(a p) k -> p a k", p=P))
+        xsrc = {}
+
+        def load_x(r, pieces):
+            b = r // (TPP // RT)
+            t0 = RT * (r % (TPP // RT))
+            view = tensor[b].rearrange("(p t) k -> p t k", t=TPP)
+            n = RT // pieces
+            for c in range(pieces):
+                xt = xpool.tile([P, n, HID], BF16, name="x%d_%d" % (r, c))
+                nc.sync.dma_start(out=xt[:], in_=view[:, t0 + c * n:t0 + (c + 1) * n, :])
+                for j in range(n):
+                    xsrc[(r, c * n + j)] = xt[:, j, :]
+
+        load_x(0, 2)
+        pe_sb = const.tile([P, TPP, 128], BF16, name="pe_sb")
+        nc.sync.dma_start(out=pe_sb[:], in_=pos_emb.rearrange("(p t) c -> p t c", t=TPP))
+        for r in range(1, ROUNDS):
+            load_x(r, 1)
+
+        ident_f = const.tile([P, P], F32, name="ident_f")
+        make_identity(nc, ident_f[:])
+        ident_b = const.tile([P, P], BF16, name="ident_b")
+        make_identity(nc, ident_b[:])
+
+        ta = const.tile([P, 3, 64], BF16, name="ta")
+        nc.vector.tensor_tensor(
+            out=ta[:], in0=bb[:, 0:192].rearrange("p (h d) -> p h d", h=3),
+            in1=ident_b[:, 0:64].unsqueeze(1).to_broadcast([P, 3, 64]), op=MULT)
+        tb = const.tile([P, 3, 32, 2], BF16, name="tb")
+        bbv = bb[:, 0:192].rearrange("p (h i e) -> p h i e", h=3, e=2)
+        idv = ident_b[:, 64:128].rearrange("p (i e) -> p i e", e=2)
+        for e in range(2):
+            nc.vector.tensor_tensor(
+                out=tb[:, :, :, e], in0=bbv[:, :, :, 1 - e],
+                in1=idv[:, :, e].unsqueeze(1).to_broadcast([P, 3, 32]), op=MULT)
+        mb = const.tile([P, 192], BF16, name="mb")
+        nc.vector.tensor_tensor(
+            out=mb[:], in0=ta[:].rearrange("p h d -> p (h d)"),
+            in1=tb[:].rearrange("p h i e -> p (h i e)"), op=ADD)
+
+        wg = const.tile([P, 2048], BF16, name="wg", align_bytes=64)
+        wg_f = wg[:].bitcast(F32).rearrange("p (g n u) -> p g n u", g=2, u=2)
+        for a in range(2):
+            tw = psum.tile([P, 512], F32, tag="T%d" % a, name="tw%d" % a)
+            wa = w_sb[:, a, :].bitcast(F32)
+            for q in range(4):
+                nc.tensor.transpose(tw[:, 128 * q:128 * (q + 1)], wa[:, 128 * q:128 * (q + 1)], ident_f[:])
+            nc.scalar.copy(out=wg_f[:, :, 128 * a:128 * (a + 1), :],
+                           in_=tw[:].rearrange("p (g u n) -> p g n u", g=2, u=2))
+        wc = const.tile([P, 512], U32, name="wc", align_bytes=64)
+        ws = const.tile([P, 512], U8, name="ws", align_bytes=64)
+        nc.vector.quantize_mx(out=wc[:].bitcast(FP8X4), scales=ws[:], in_=wg[:])
+
+        tbank = {}
+        grp = {}
+        codes = {}
+        xbank = {}
+        ystage = {}
+
+        def transposes(r):
+            for i in range(RT):
+                tt = psum.tile([P, 512], F32, tag="T%d" % i, name="T%d_%d" % (i, r))
+                xa = xsrc[(r, i)].bitcast(F32)
+                for q in range(4):
+                    nc.tensor.transpose(tt[:, 128 * q:128 * (q + 1)], xa[:, 128 * q:128 * (q + 1)], ident_f[:])
+                tbank[(r, i)] = tt
+
+        def copies(r):
+            g = gpool.tile([P, RT * HID], BF16, tag="grp", name="grp%d" % r, align_bytes=64)
+            gf = g[:].bitcast(F32).rearrange("p (i g r u) -> p i g r u", i=RT, g=2, u=2)
+            for i in range(RT):
+                nc.scalar.copy(out=gf[:, i], in_=tbank[(r, i)][:].rearrange("p (g u r) -> p g r u", g=2, u=2))
+            grp[r] = g
+
+        def quant(r):
+            c = cpool.tile([P, RT * 256], U32, tag="codes", name="codes%d" % r, align_bytes=64)
+            s = cpool.tile([P, RT * 256], U8, tag="scl", name="scl%d" % r, align_bytes=64)
+            nc.vector.quantize_mx(out=c[:].bitcast(FP8X4), scales=s[:], in_=grp[r][:])
+            codes[r] = (c, s)
+
+        def mx(r, u):
+            c, s = codes[r]
+            t0 = RT * (r % (TPP // RT))
+            xb = psum.tile([P, 2, 256], F32, tag="X%d" % u, name="X%d_%d" % (u, r))
+            for tt in range(2):
+                i = 2 * u + tt
+                for g in range(2):
+                    lo = (2 * i + g) * 128
+                    nc.tensor.matmul_mx(
+                        out=xb[:, tt, :],
+                        lhsT=c[:, lo:lo + 128].bitcast(FP8X4), lhsT_scale=s[:, lo:lo + 128],
+                        rhs=wc[:, 256 * g:256 * (g + 1)].bitcast(FP8X4), rhs_scale=ws[:, 256 * g:256 * (g + 1)],
+                        start=(g == 0), stop=(g == 1))
+            rb = psum.tile([P, 2, 256], F32, tag="R%d" % u, name="R%d_%d" % (u, r))
+            for tt in range(2):
+                nc.tensor.matmul(out=rb[:, tt, 0:192], lhsT=peT[:, t0 + 2 * u + tt, :], rhs=mb[:],
+                                 start=True, stop=True)
+            xbank[(r, u)] = (xb, rb)
+
+        def group_of(b, t):
+            if b == NB - 1 and t >= 8:
+                return (8, 12) if t < 12 else (12, 16)
+            return (0, 8) if t < 8 else (8, 16)
+
+        def rope(r, u):
+            b = r // (TPP // RT)
+            t = RT * (r % (TPP // RT)) + 2 * u
+            g0, g1 = group_of(b, t)
+            if t == g0:
+                ystage[b] = ypool.tile([P, 4, g1 - g0, 64], F32, tag="ys", name="ys%d_%d" % (b, g0))
+            ys = ystage[b]
+            tl = t - g0
+            xb, rb = xbank[(r, u)]
+            m1 = mpool.tile([P, 2, 3, 64], F32, tag="m1", name="m1_%d_%d" % (r, u))
+            pl = mpool.tile([P, 2, 2, 3, 32], F32, tag="pl", name="pl_%d_%d" % (r, u))
+            xr = xb[:, :, 0:192]
+            nc.vector.tensor_tensor(
+                out=m1[:], in0=xr.rearrange("p t (h d) -> p t h d", h=3),
+                in1=pe_sb[:, t:t + 2, 0:64].unsqueeze(2).to_broadcast([P, 2, 3, 64]), op=MULT)
+            xe = xr.rearrange("p t (h i e) -> p t h i e", h=3, e=2)
+            se = pe_sb[:, t:t + 2, 64:128].rearrange("p t (i e) -> p t i e", e=2)
+            for e in range(2):
+                nc.vector.tensor_tensor(
+                    out=pl[:, e], in0=xe[:, :, :, :, 1 - e],
+                    in1=se[:, :, :, e].unsqueeze(2).to_broadcast([P, 2, 3, 32]), op=MULT)
+            if V_OFF_VECTOR:
+                nc.scalar.copy(out=ys[:, 3, tl:tl + 2, :], in_=xb[:, :, 192:256])
+            else:
+                nc.vector.tensor_tensor(
+                    out=ys[:, 3, tl:tl + 2, :], in0=xb[:, :, 192:256],
+                    in1=bb[:, 192:256].unsqueeze(1).to_broadcast([P, 2, 64]), op=ADD)
+            nc.vector.tensor_tensor(
+                out=m1[:], in0=m1[:], in1=rb[:, :, 0:192].rearrange("p t (h d) -> p t h d", h=3), op=ADD)
+            eng = nc.gpsimd if A2_GPSIMD else nc.vector
+            eng.tensor_tensor(
+                out=ys[:, 0:3, tl:tl + 2, :].rearrange("p h t (i e) -> p t h i e", e=2),
+                in0=m1[:].rearrange("p t h (i e) -> p t h i e", e=2),
+                in1=pl[:].rearrange("p e t h i -> p t h i e"), op=ADD)
+            if t + 2 == g1:
+                if V_OFF_VECTOR:
+                    nc.gpsimd.tensor_tensor(
+                        out=ys[:, 3, :, :], in0=ys[:, 3, :, :],
+                        in1=bb[:, 192:256].unsqueeze(1).to_broadcast([P, g1 - g0, 64]), op=ADD)
+                nc.sync.dma_start(out=out_0[b].rearrange("h (p t) d -> p h t d", t=TPP)[:, :, g0:g1, :],
+                                  in_=ys[:, 0:2, :, :])
+                nc.sync.dma_start(out=out_1[b, 0].rearrange("(p t) d -> p t d", t=TPP)[:, g0:g1, :],
+                                  in_=ys[:, 2, :, :])
+                nc.sync.dma_start(out=out_2[b, 0].rearrange("(p t) d -> p t d", t=TPP)[:, g0:g1, :],
+                                  in_=ys[:, 3, :, :])
+
+        transposes(0)
+        copies(0)
+        peT = const.tile([P, TPP, 128], BF16, name="peT")
+        for hf in range(2):
+            tp = psum.tile([P, 8, 128], BF16, tag="R%d" % hf, name="tp%d" % hf)
+            for j in range(8):
+                nc.tensor.transpose(tp[:, j, :], pe_sb[:, 8 * hf + j, :], ident_b[:])
+            nc.scalar.copy(out=peT[:, 8 * hf:8 * (hf + 1), :], in_=tp[:])
+        for r in range(ROUNDS + 1):
+            if r + 1 < ROUNDS:
+                transposes(r + 1)
+                copies(r + 1)
+            if r < ROUNDS:
+                quant(r)
+            for u in range(2):
+                if r >= 1:
+                    rope(r - 1, u)
+                if r < ROUNDS:
+                    mx(r, u)

@@ -21,7 +21,7 @@ RT = 4
 ROUNDS = NB * TPP // RT
 
 MANUAL = True
-A2_GPSIMD = True
+A2_GPSIMD = False
 V_OFF_VECTOR = False
 
 

@@ -17,12 +17,14 @@ P = 128
 NB = 4
 TPP = 16
 HID = 1024
-RT = 4
-ROUNDS = NB * TPP // RT
+UPB = TPP // 2
+NU = NB * UPB
 
 MANUAL = True
-A2_GPSIMD = False
-V_OFF_VECTOR = False
+REV = True
+V_OFF_VECTOR = True
+A1G_MOD = 2
+TAIL_ON_VECTOR = True
 
 
 def tile_multiqueryattention_pa_t_kernel(tc, tensor, w_qkv, b_qkv, pos_emb, out_0, out_1, out_2):
@@ -30,13 +32,16 @@ def tile_multiqueryattention_pa_t_kernel(tc, tensor, w_qkv, b_qkv, pos_emb, out_
     with ExitStack() as ctx:
         const = ctx.enter_context(tc.tile_pool(name="const", bufs=1))
         xpool = ctx.enter_context(tc.tile_pool(name="xpool", bufs=1))
-        gpool = ctx.enter_context(tc.tile_pool(name="gpool", bufs=2))
-        cpool = ctx.enter_context(tc.tile_pool(name="cpool", bufs=2))
-        mpool = ctx.enter_context(tc.tile_pool(name="mpool", bufs=4))
+        gpool = ctx.enter_context(tc.tile_pool(name="gpool", bufs=3))
+        cpool = ctx.enter_context(tc.tile_pool(name="cpool", bufs=3))
+        mpool = ctx.enter_context(tc.tile_pool(name="mpool", bufs=5))
         ypool = ctx.enter_context(tc.tile_pool(name="ypool", bufs=3))
         psum = ctx.enter_context(tc.psum_pool(name="psum", bufs=1))
         if MANUAL:
             ctx.enter_context(tc.manual_schedule())
+
+        def a1_on_gpsimd(n):
+            return A1G_MOD == 2 and n % 2 == 1 and not (TAIL_ON_VECTOR and n == NU - 1)
 
         bb = const.tile([P, 256], BF16, name="bb")
         nc.scalar.dma_start(out=bb[:], in_=b_qkv.partition_broadcast(P))
@@ -44,22 +49,21 @@ def tile_multiqueryattention_pa_t_kernel(tc, tensor, w_qkv, b_qkv, pos_emb, out_
         nc.sync.dma_start(out=w_sb[:], in_=w_qkv.rearrange("(a p) k -> p a k", p=P))
         xsrc = {}
 
-        def load_x(r, pieces):
-            b = r // (TPP // RT)
-            t0 = RT * (r % (TPP // RT))
+        def load_x(n0, units):
+            b = n0 // UPB
+            t0 = 2 * (n0 % UPB)
             view = tensor[b].rearrange("(p t) k -> p t k", t=TPP)
-            n = RT // pieces
-            for c in range(pieces):
-                xt = xpool.tile([P, n, HID], BF16, name="x%d_%d" % (r, c))
-                nc.sync.dma_start(out=xt[:], in_=view[:, t0 + c * n:t0 + (c + 1) * n, :])
-                for j in range(n):
-                    xsrc[(r, c * n + j)] = xt[:, j, :]
+            xt = xpool.tile([P, 2 * units, HID], BF16, name="x%d" % n0)
+            nc.sync.dma_start(out=xt[:], in_=view[:, t0:t0 + 2 * units, :])
+            for j in range(2 * units):
+                xsrc[(n0 + j // 2, j % 2)] = xt[:, j, :]
 
-        load_x(0, 2)
+        load_x(0, 1)
+        load_x(1, 1)
         pe_sb = const.tile([P, TPP, 128], BF16, name="pe_sb")
         nc.sync.dma_start(out=pe_sb[:], in_=pos_emb.rearrange("(p t) c -> p t c", t=TPP))
-        for r in range(1, ROUNDS):
-            load_x(r, 1)
+        for n0 in range(2, NU, 2):
+            load_x(n0, 2)
 
         ident_f = const.tile([P, P], F32, name="ident_f")
         make_identity(nc, ident_f[:])
@@ -85,101 +89,142 @@ def tile_multiqueryattention_pa_t_kernel(tc, tensor, w_qkv, b_qkv, pos_emb, out_
         wg = const.tile([P, 2048], BF16, name="wg", align_bytes=64)
         wg_f = wg[:].bitcast(F32).rearrange("p (g n u) -> p g n u", g=2, u=2)
         for a in range(2):
-            tw = psum.tile([P, 512], F32, tag="T%d" % a, name="tw%d" % a)
+            tw = psum.tile([P, 512], F32, tag="T%d" % (2 + a), name="tw%d" % a)
             wa = w_sb[:, a, :].bitcast(F32)
             for q in range(4):
                 nc.tensor.transpose(tw[:, 128 * q:128 * (q + 1)], wa[:, 128 * q:128 * (q + 1)], ident_f[:])
-            nc.scalar.copy(out=wg_f[:, :, 128 * a:128 * (a + 1), :],
-                           in_=tw[:].rearrange("p (g u n) -> p g n u", g=2, u=2))
+            src = tw[:].rearrange("p (g u n) -> p g n u", g=2, u=2)
+            if a == 0:
+                nc.scalar.copy(out=wg_f[:, :, 0:128, :], in_=src)
+            else:
+                nc.vector.tensor_copy(out=wg_f[:, :, 128:256, :], in_=src)
         wc = const.tile([P, 512], U32, name="wc", align_bytes=64)
         ws = const.tile([P, 512], U8, name="ws", align_bytes=64)
         nc.vector.quantize_mx(out=wc[:].bitcast(FP8X4), scales=ws[:], in_=wg[:])
+
+        rbs = const.tile([P, UPB // 2, 2, 192], F32, name="rbs")
+        peT = const.tile([P, TPP, 128], BF16, name="peT")
 
         tbank = {}
         grp = {}
         codes = {}
         xbank = {}
+        rbank = {}
+        work = {}
         ystage = {}
+        rcount = [0]
 
-        def transposes(r):
-            for i in range(RT):
-                tt = psum.tile([P, 512], F32, tag="T%d" % i, name="T%d_%d" % (i, r))
-                xa = xsrc[(r, i)].bitcast(F32)
-                for q in range(4):
-                    nc.tensor.transpose(tt[:, 128 * q:128 * (q + 1)], xa[:, 128 * q:128 * (q + 1)], ident_f[:])
-                tbank[(r, i)] = tt
-
-        def copies(r):
-            g = gpool.tile([P, RT * HID], BF16, tag="grp", name="grp%d" % r, align_bytes=64)
-            gf = g[:].bitcast(F32).rearrange("p (i g r u) -> p i g r u", i=RT, g=2, u=2)
-            for i in range(RT):
-                nc.scalar.copy(out=gf[:, i], in_=tbank[(r, i)][:].rearrange("p (g u r) -> p g r u", g=2, u=2))
-            grp[r] = g
-
-        def quant(r):
-            c = cpool.tile([P, RT * 256], U32, tag="codes", name="codes%d" % r, align_bytes=64)
-            s = cpool.tile([P, RT * 256], U8, tag="scl", name="scl%d" % r, align_bytes=64)
-            nc.vector.quantize_mx(out=c[:].bitcast(FP8X4), scales=s[:], in_=grp[r][:])
-            codes[r] = (c, s)
-
-        def mx(r, u):
-            c, s = codes[r]
-            t0 = RT * (r % (TPP // RT))
-            xb = psum.tile([P, 2, 256], F32, tag="X%d" % u, name="X%d_%d" % (u, r))
+        def transposes(n):
             for tt in range(2):
-                i = 2 * u + tt
+                tp = psum.tile([P, 512], F32, tag="T%d" % ((2 * n + tt) % 4), name="T%d_%d" % (tt, n))
+                xa = xsrc[(n, tt)].bitcast(F32)
+                for q in range(4):
+                    nc.tensor.transpose(tp[:, 128 * q:128 * (q + 1)], xa[:, 128 * q:128 * (q + 1)], ident_f[:])
+                tbank[(n, tt)] = tp
+
+        def copies(n):
+            g = gpool.tile([P, 2 * HID], BF16, tag="grp", name="grp%d" % n, align_bytes=64)
+            gf = g[:].bitcast(F32).rearrange("p (i g r u) -> p i g r u", i=2, g=2, u=2)
+            for tt in range(2):
+                nc.scalar.copy(out=gf[:, tt], in_=tbank[(n, tt)][:].rearrange("p (g u r) -> p g r u", g=2, u=2))
+            grp[n] = g
+
+        def quant(n):
+            c = cpool.tile([P, 512], U32, tag="codes", name="codes%d" % n, align_bytes=64)
+            s = cpool.tile([P, 512], U8, tag="scl", name="scl%d" % n, align_bytes=64)
+            nc.vector.quantize_mx(out=c[:].bitcast(FP8X4), scales=s[:], in_=grp[n][:])
+            codes[n] = (c, s)
+
+        def mx(n):
+            c, s = codes[n]
+            xb = psum.tile([P, 2, 256], F32, tag="X%d" % (n % 2), name="X_%d" % n)
+            for tt in range(2):
                 for g in range(2):
-                    lo = (2 * i + g) * 128
+                    lo = (2 * tt + g) * 128
                     nc.tensor.matmul_mx(
                         out=xb[:, tt, :],
                         lhsT=c[:, lo:lo + 128].bitcast(FP8X4), lhsT_scale=s[:, lo:lo + 128],
                         rhs=wc[:, 256 * g:256 * (g + 1)].bitcast(FP8X4), rhs_scale=ws[:, 256 * g:256 * (g + 1)],
                         start=(g == 0), stop=(g == 1))
-            rb = psum.tile([P, 2, 256], F32, tag="R%d" % u, name="R%d_%d" % (u, r))
+            xbank[n] = xb
+
+        def rbmm(n):
+            if a1_on_gpsimd(n) and n >= UPB:
+                return
+            t = 2 * (n % UPB)
+            rb = psum.tile([P, 2, 256], F32, tag="R%d" % (rcount[0] % 2), name="R_%d" % n)
+            rcount[0] += 1
             for tt in range(2):
-                nc.tensor.matmul(out=rb[:, tt, 0:192], lhsT=peT[:, t0 + 2 * u + tt, :], rhs=mb[:],
-                                 start=True, stop=True)
-            xbank[(r, u)] = (xb, rb)
+                nc.tensor.matmul(out=rb[:, tt, 0:192], lhsT=peT[:, t + tt, :], rhs=mb[:], start=True, stop=True)
+            if a1_on_gpsimd(n):
+                nc.scalar.copy(out=rbs[:, (n % UPB) // 2], in_=rb[:, :, 0:192])
+            else:
+                rbank[n] = rb
 
         def group_of(b, t):
             if b == NB - 1 and t >= 8:
                 return (8, 12) if t < 12 else (12, 16)
             return (0, 8) if t < 8 else (8, 16)
 
-        def rope(r, u):
-            b = r // (TPP // RT)
-            t = RT * (r % (TPP // RT)) + 2 * u
+        def rope_mul(n):
+            b = n // UPB
+            t = 2 * (n % UPB)
             g0, g1 = group_of(b, t)
             if t == g0:
                 ystage[b] = ypool.tile([P, 4, g1 - g0, 64], F32, tag="ys", name="ys%d_%d" % (b, g0))
             ys = ystage[b]
             tl = t - g0
-            xb, rb = xbank[(r, u)]
-            m1 = mpool.tile([P, 2, 3, 64], F32, tag="m1", name="m1_%d_%d" % (r, u))
-            pl = mpool.tile([P, 2, 2, 3, 32], F32, tag="pl", name="pl_%d_%d" % (r, u))
+            xb = xbank[n]
+            m1 = mpool.tile([P, 2, 3, 64], F32, tag="m1", name="m1_%d" % n)
             xr = xb[:, :, 0:192]
             nc.vector.tensor_tensor(
                 out=m1[:], in0=xr.rearrange("p t (h d) -> p t h d", h=3),
                 in1=pe_sb[:, t:t + 2, 0:64].unsqueeze(2).to_broadcast([P, 2, 3, 64]), op=MULT)
             xe = xr.rearrange("p t (h i e) -> p t h i e", h=3, e=2)
             se = pe_sb[:, t:t + 2, 64:128].rearrange("p t (i e) -> p t i e", e=2)
-            for e in range(2):
+            if REV:
+                pl = mpool.tile([P, 2, 3, 64], F32, tag="pl", name="pl_%d" % n)
                 nc.vector.tensor_tensor(
-                    out=pl[:, e], in0=xe[:, :, :, :, 1 - e],
-                    in1=se[:, :, :, e].unsqueeze(2).to_broadcast([P, 2, 3, 32]), op=MULT)
+                    out=pl[:].rearrange("p t h (i e) -> p t h i e", e=2), in0=xe[:, :, :, :, ::-1],
+                    in1=se.unsqueeze(2).to_broadcast([P, 2, 3, 32, 2]), op=MULT)
+            else:
+                pl = mpool.tile([P, 2, 2, 3, 32], F32, tag="pl", name="pl_%d" % n)
+                for e in range(2):
+                    nc.vector.tensor_tensor(
+                        out=pl[:, e], in0=xe[:, :, :, :, 1 - e],
+                        in1=se[:, :, :, e].unsqueeze(2).to_broadcast([P, 2, 3, 32]), op=MULT)
             if V_OFF_VECTOR:
                 nc.scalar.copy(out=ys[:, 3, tl:tl + 2, :], in_=xb[:, :, 192:256])
             else:
                 nc.vector.tensor_tensor(
                     out=ys[:, 3, tl:tl + 2, :], in0=xb[:, :, 192:256],
                     in1=bb[:, 192:256].unsqueeze(1).to_broadcast([P, 2, 64]), op=ADD)
-            nc.vector.tensor_tensor(
-                out=m1[:], in0=m1[:], in1=rb[:, :, 0:192].rearrange("p t (h d) -> p t h d", h=3), op=ADD)
-            eng = nc.gpsimd if A2_GPSIMD else nc.vector
-            eng.tensor_tensor(
-                out=ys[:, 0:3, tl:tl + 2, :].rearrange("p h t (i e) -> p t h i e", e=2),
-                in0=m1[:].rearrange("p t h (i e) -> p t h i e", e=2),
-                in1=pl[:].rearrange("p e t h i -> p t h i e"), op=ADD)
+            work[n] = (m1, pl)
+
+        def rope_add(n):
+            b = n // UPB
+            t = 2 * (n % UPB)
+            g0, g1 = group_of(b, t)
+            ys = ystage[b]
+            tl = t - g0
+            m1, pl = work[n]
+            if a1_on_gpsimd(n):
+                nc.gpsimd.tensor_tensor(
+                    out=m1[:], in0=m1[:],
+                    in1=rbs[:, (n % UPB) // 2].rearrange("p t (h d) -> p t h d", h=3), op=ADD)
+            else:
+                nc.vector.tensor_tensor(
+                    out=m1[:], in0=m1[:], in1=rbank[n][:, :, 0:192].rearrange("p t (h d) -> p t h d", h=3), op=ADD)
+            eng = nc.vector if (TAIL_ON_VECTOR and n == NU - 1) else nc.gpsimd
+            if REV:
+                eng.tensor_tensor(
+                    out=ys[:, 0:3, tl:tl + 2, :].rearrange("p h t d -> p t h d"),
+                    in0=m1[:], in1=pl[:], op=ADD)
+            else:
+                eng.tensor_tensor(
+                    out=ys[:, 0:3, tl:tl + 2, :].rearrange("p h t (i e) -> p t h i e", e=2),
+                    in0=m1[:].rearrange("p t h (i e) -> p t h i e", e=2),
+                    in1=pl[:].rearrange("p e t h i -> p t h i e"), op=ADD)
             if t + 2 == g1:
                 if V_OFF_VECTOR:
                     nc.gpsimd.tensor_tensor(
@@ -192,22 +237,22 @@ def tile_multiqueryattention_pa_t_kernel(tc, tensor, w_qkv, b_qkv, pos_emb, out_
                 nc.sync.dma_start(out=out_2[b, 0].rearrange("(p t) d -> p t d", t=TPP)[:, g0:g1, :],
                                   in_=ys[:, 3, :, :])
 
-        transposes(0)
-        copies(0)
-        peT = const.tile([P, TPP, 128], BF16, name="peT")
-        for hf in range(2):
-            tp = psum.tile([P, 8, 128], BF16, tag="R%d" % hf, name="tp%d" % hf)
-            for j in range(8):
-                nc.tensor.transpose(tp[:, j, :], pe_sb[:, 8 * hf + j, :], ident_b[:])
-            nc.scalar.copy(out=peT[:, 8 * hf:8 * (hf + 1), :], in_=tp[:])
-        for r in range(ROUNDS + 1):
-            if r + 1 < ROUNDS:
-                transposes(r + 1)
-                copies(r + 1)
-            if r < ROUNDS:
-                quant(r)
-            for u in range(2):
-                if r >= 1:
-                    rope(r - 1, u)
-                if r < ROUNDS:
-                    mx(r, u)
+        for s in range(-2, NU):
+            if s + 2 < NU:
+                transposes(s + 2)
+                copies(s + 2)
+            if s == -1:
+                for hf in range(2):
+                    tq = psum.tile([P, 8, 128], BF16, tag="R%d" % hf, name="tq%d" % hf)
+                    for j in range(8):
+                        nc.tensor.transpose(tq[:, j, :], pe_sb[:, 8 * hf + j, :], ident_b[:])
+                    nc.scalar.copy(out=peT[:, 8 * hf:8 * (hf + 1), :], in_=tq[:])
+            if 0 <= s + 1 < NU:
+                quant(s + 1)
+            if s >= 0:
+                rope_mul(s)
+            if 0 <= s + 1 < NU:
+                mx(s + 1)
+                rbmm(s + 1)
+            if s >= 0:
+                rope_add(s)

@@ -23,7 +23,7 @@ NU = NB * UPB
 MANUAL = True
 REV = True
 V_OFF_VECTOR = True
-A1G_MOD = 2
+A1G_MOD = 0
 TAIL_ON_VECTOR = True
 
 
@@ -102,7 +102,7 @@ def tile_multiqueryattention_pa_t_kernel(tc, tensor, w_qkv, b_qkv, pos_emb, out_
         ws = const.tile([P, 512], U8, name="ws", align_bytes=64)
         nc.vector.quantize_mx(out=wc[:].bitcast(FP8X4), scales=ws[:], in_=wg[:])
 
-        rbs = const.tile([P, UPB // 2, 2, 192], F32, name="rbs")
+        rbs = const.tile([P, UPB // 2, 2, 192], F32, name="rbs") if A1G_MOD == 2 else None
         peT = const.tile([P, TPP, 128], BF16, name="peT")
 
         tbank = {}
@@ -241,18 +241,18 @@ def tile_multiqueryattention_pa_t_kernel(tc, tensor, w_qkv, b_qkv, pos_emb, out_
             if s + 2 < NU:
                 transposes(s + 2)
                 copies(s + 2)
-            if s == -1:
-                for hf in range(2):
-                    tq = psum.tile([P, 8, 128], BF16, tag="R%d" % hf, name="tq%d" % hf)
-                    for j in range(8):
-                        nc.tensor.transpose(tq[:, j, :], pe_sb[:, 8 * hf + j, :], ident_b[:])
-                    nc.scalar.copy(out=peT[:, 8 * hf:8 * (hf + 1), :], in_=tq[:])
             if 0 <= s + 1 < NU:
                 quant(s + 1)
             if s >= 0:
                 rope_mul(s)
             if 0 <= s + 1 < NU:
                 mx(s + 1)
+                if s == -1:
+                    for hf in range(2):
+                        tq = psum.tile([P, 8, 128], BF16, tag="R%d" % hf, name="tq%d" % hf)
+                        for j in range(8):
+                            nc.tensor.transpose(tq[:, j, :], pe_sb[:, 8 * hf + j, :], ident_b[:])
+                        nc.scalar.copy(out=peT[:, 8 * hf:8 * (hf + 1), :], in_=tq[:])
                 rbmm(s + 1)
             if s >= 0:
                 rope_add(s)

@@ -25,6 +25,8 @@ REV = True
 V_OFF_VECTOR = True
 A1G_MOD = 0
 TAIL_ON_VECTOR = True
+AHEAD = 3
+DUMMY = 2
 
 
 def tile_multiqueryattention_pa_t_kernel(tc, tensor, w_qkv, b_qkv, pos_emb, out_0, out_1, out_2):
@@ -32,7 +34,7 @@ def tile_multiqueryattention_pa_t_kernel(tc, tensor, w_qkv, b_qkv, pos_emb, out_
     with ExitStack() as ctx:
         const = ctx.enter_context(tc.tile_pool(name="const", bufs=1))
         xpool = ctx.enter_context(tc.tile_pool(name="xpool", bufs=1))
-        gpool = ctx.enter_context(tc.tile_pool(name="gpool", bufs=3))
+        gpool = ctx.enter_context(tc.tile_pool(name="gpool", bufs=AHEAD + 1))
         cpool = ctx.enter_context(tc.tile_pool(name="cpool", bufs=3))
         mpool = ctx.enter_context(tc.tile_pool(name="mpool", bufs=5))
         ypool = ctx.enter_context(tc.tile_pool(name="ypool", bufs=3))
@@ -117,10 +119,16 @@ def tile_multiqueryattention_pa_t_kernel(tc, tensor, w_qkv, b_qkv, pos_emb, out_
         def transposes(n):
             for tt in range(2):
                 tp = psum.tile([P, 512], F32, tag="T%d" % ((2 * n + tt) % 4), name="T%d_%d" % (tt, n))
+                tbank[(n, tt)] = tp
+                if n >= 4 and tt < DUMMY:
+                    nc.tensor.matmul_mx(
+                        out=tp[:], lhsT=wc[:, 0:128].bitcast(FP8X4), lhsT_scale=ws[:, 0:128],
+                        rhs=wc[:].bitcast(FP8X4), rhs_scale=ws[:], start=True, stop=True)
+            for tt in range(2):
+                tp = tbank[(n, tt)]
                 xa = xsrc[(n, tt)].bitcast(F32)
                 for q in range(4):
                     nc.tensor.transpose(tp[:, 128 * q:128 * (q + 1)], xa[:, 128 * q:128 * (q + 1)], ident_f[:])
-                tbank[(n, tt)] = tp
 
         def copies(n):
             g = gpool.tile([P, 2 * HID], BF16, tag="grp", name="grp%d" % n, align_bytes=64)
@@ -237,10 +245,11 @@ def tile_multiqueryattention_pa_t_kernel(tc, tensor, w_qkv, b_qkv, pos_emb, out_
                 nc.sync.dma_start(out=out_2[b, 0].rearrange("(p t) d -> p t d", t=TPP)[:, g0:g1, :],
                                   in_=ys[:, 3, :, :])
 
-        for s in range(-2, NU):
-            if s + 2 < NU:
-                transposes(s + 2)
-                copies(s + 2)
+        for s in range(-AHEAD, NU):
+            late = -1 <= s <= 0
+            if s + AHEAD < NU and not late:
+                transposes(s + AHEAD)
+                copies(s + AHEAD)
             if 0 <= s + 1 < NU:
                 quant(s + 1)
             if s >= 0:
@@ -256,3 +265,6 @@ def tile_multiqueryattention_pa_t_kernel(tc, tensor, w_qkv, b_qkv, pos_emb, out_
                 rbmm(s + 1)
             if s >= 0:
                 rope_add(s)
+            if late:
+                transposes(s + AHEAD)
+                copies(s + AHEAD)

@@ -12,6 +12,7 @@ U8 = mybir.dt.uint8
 FP8X4 = mybir.dt.float8_e4m3fn_x4
 ADD = mybir.AluOpType.add
 MULT = mybir.AluOpType.mult
+IDENT = mybir.ActivationFunctionType.Identity
 
 P = 128
 NB = 4
@@ -21,12 +22,8 @@ UPB = TPP // 2
 NU = NB * UPB
 
 MANUAL = True
-REV = True
-V_OFF_VECTOR = True
-A1G_MOD = 0
+V_COPY_ON_VECTOR = True
 TAIL_ON_VECTOR = True
-AHEAD = 3
-DUMMY = 2
 
 
 def tile_multiqueryattention_pa_t_kernel(tc, tensor, w_qkv, b_qkv, pos_emb, out_0, out_1, out_2):
@@ -34,16 +31,21 @@ def tile_multiqueryattention_pa_t_kernel(tc, tensor, w_qkv, b_qkv, pos_emb, out_
     with ExitStack() as ctx:
         const = ctx.enter_context(tc.tile_pool(name="const", bufs=1))
         xpool = ctx.enter_context(tc.tile_pool(name="xpool", bufs=1))
-        gpool = ctx.enter_context(tc.tile_pool(name="gpool", bufs=AHEAD + 1))
-        cpool = ctx.enter_context(tc.tile_pool(name="cpool", bufs=3))
-        mpool = ctx.enter_context(tc.tile_pool(name="mpool", bufs=5))
+        gpool = ctx.enter_context(tc.tile_pool(name="gpool", bufs=2))
+        cpool = ctx.enter_context(tc.tile_pool(name="cpool", bufs=2))
+        epool = ctx.enter_context(tc.tile_pool(name="epool", bufs=2))
+        mpool = ctx.enter_context(tc.tile_pool(name="mpool", bufs=4))
         ypool = ctx.enter_context(tc.tile_pool(name="ypool", bufs=3))
         psum = ctx.enter_context(tc.psum_pool(name="psum", bufs=1))
         if MANUAL:
             ctx.enter_context(tc.manual_schedule())
 
-        def a1_on_gpsimd(n):
-            return A1G_MOD == 2 and n % 2 == 1 and not (TAIL_ON_VECTOR and n == NU - 1)
+        groups = [[0], [1]] + [[n, n + 1] for n in range(2, NU, 2)]
+        NG = len(groups)
+        group_index = {}
+        for k in range(NG):
+            for n in groups[k]:
+                group_index[n] = k
 
         bb = const.tile([P, 256], BF16, name="bb")
         nc.scalar.dma_start(out=bb[:], in_=b_qkv.partition_broadcast(P))
@@ -69,24 +71,26 @@ def tile_multiqueryattention_pa_t_kernel(tc, tensor, w_qkv, b_qkv, pos_emb, out_
 
         ident_f = const.tile([P, P], F32, name="ident_f")
         make_identity(nc, ident_f[:])
-        ident_b = const.tile([P, P], BF16, name="ident_b")
-        make_identity(nc, ident_b[:])
 
-        ta = const.tile([P, 3, 64], BF16, name="ta")
+        bsel = const.tile([P, 2, P], F32, name="bsel")
         nc.vector.tensor_tensor(
-            out=ta[:], in0=bb[:, 0:192].rearrange("p (h d) -> p h d", h=3),
-            in1=ident_b[:, 0:64].unsqueeze(1).to_broadcast([P, 3, 64]), op=MULT)
-        tb = const.tile([P, 3, 32, 2], BF16, name="tb")
-        bbv = bb[:, 0:192].rearrange("p (h i e) -> p h i e", h=3, e=2)
-        idv = ident_b[:, 64:128].rearrange("p (i e) -> p i e", e=2)
-        for e in range(2):
-            nc.vector.tensor_tensor(
-                out=tb[:, :, :, e], in0=bbv[:, :, :, 1 - e],
-                in1=idv[:, :, e].unsqueeze(1).to_broadcast([P, 3, 32]), op=MULT)
-        mb = const.tile([P, 192], BF16, name="mb")
-        nc.vector.tensor_tensor(
-            out=mb[:], in0=ta[:].rearrange("p h d -> p (h d)"),
-            in1=tb[:].rearrange("p h i e -> p (h i e)"), op=ADD)
+            out=bsel[:], in0=bb[:].rearrange("p (f j) -> p f j", f=2),
+            in1=ident_f[:].unsqueeze(1).to_broadcast([P, 2, P]), op=MULT)
+        bcol = const.tile([P, 2], F32, name="bcol")
+        nc.vector.tensor_reduce(out=bcol[:], in_=bsel[:], axis=mybir.AxisListType.X, op=ADD)
+
+        tab = const.tile([P, TPP, 2, 64], BF16, name="tab")
+
+        def build_tab(ta0, ta1):
+            cos_src = pe_sb[:, ta0:ta1, 0:64]
+            sin_src = pe_sb[:, ta0:ta1, 64:128].rearrange("p t (i e) -> p t i e", e=2)[:, :, :, ::-1]
+            sin_dst = tab[:, ta0:ta1, 1, :].rearrange("p t (i e) -> p t i e", e=2)
+            nc.gpsimd.tensor_scalar(out=tab[:, ta0:ta1, 0, :], in0=cos_src, scalar1=1.0, scalar2=0.0,
+                                    op0=MULT, op1=ADD)
+            nc.gpsimd.tensor_scalar(out=sin_dst, in0=sin_src, scalar1=1.0, scalar2=0.0, op0=MULT, op1=ADD)
+
+        build_tab(0, 4)
+        build_tab(4, TPP)
 
         wg = const.tile([P, 2048], BF16, name="wg", align_bytes=64)
         wg_f = wg[:].bitcast(F32).rearrange("p (g n u) -> p g n u", g=2, u=2)
@@ -104,77 +108,77 @@ def tile_multiqueryattention_pa_t_kernel(tc, tensor, w_qkv, b_qkv, pos_emb, out_
         ws = const.tile([P, 512], U8, name="ws", align_bytes=64)
         nc.vector.quantize_mx(out=wc[:].bitcast(FP8X4), scales=ws[:], in_=wg[:])
 
-        rbs = const.tile([P, UPB // 2, 2, 192], F32, name="rbs") if A1G_MOD == 2 else None
-        peT = const.tile([P, TPP, 128], BF16, name="peT")
-
         tbank = {}
         grp = {}
         codes = {}
-        xbank = {}
-        rbank = {}
+        fbank = {}
+        xtb = {}
+        ybank = {}
         work = {}
         ystage = {}
-        rcount = [0]
 
-        def transposes(n):
-            for tt in range(2):
-                tp = psum.tile([P, 512], F32, tag="T%d" % ((2 * n + tt) % 4), name="T%d_%d" % (tt, n))
-                tbank[(n, tt)] = tp
-                if n >= 4 and tt < DUMMY:
-                    nc.tensor.matmul_mx(
-                        out=tp[:], lhsT=wc[:, 0:128].bitcast(FP8X4), lhsT_scale=ws[:, 0:128],
-                        rhs=wc[:].bitcast(FP8X4), rhs_scale=ws[:], start=True, stop=True)
-            for tt in range(2):
-                tp = tbank[(n, tt)]
-                xa = xsrc[(n, tt)].bitcast(F32)
-                for q in range(4):
-                    nc.tensor.transpose(tp[:, 128 * q:128 * (q + 1)], xa[:, 128 * q:128 * (q + 1)], ident_f[:])
+        def transposes(k):
+            for n in groups[k]:
+                for tt in range(2):
+                    tp = psum.tile([P, 512], F32, tag="T%d" % ((2 * n + tt) % 4), name="T%d_%d" % (tt, n))
+                    xa = xsrc[(n, tt)].bitcast(F32)
+                    for q in range(4):
+                        nc.tensor.transpose(tp[:, 128 * q:128 * (q + 1)], xa[:, 128 * q:128 * (q + 1)], ident_f[:])
+                    tbank[(n, tt)] = tp
 
-        def copies(n):
-            g = gpool.tile([P, 2 * HID], BF16, tag="grp", name="grp%d" % n, align_bytes=64)
-            gf = g[:].bitcast(F32).rearrange("p (i g r u) -> p i g r u", i=2, g=2, u=2)
-            for tt in range(2):
-                nc.scalar.copy(out=gf[:, tt], in_=tbank[(n, tt)][:].rearrange("p (g u r) -> p g r u", g=2, u=2))
-            grp[n] = g
+        def copies(k):
+            tiles = 2 * len(groups[k])
+            g = gpool.tile([P, tiles * HID], BF16, tag="grp", name="grp%d" % k, align_bytes=64)
+            gf = g[:].bitcast(F32).rearrange("p (g i r u) -> p g i r u", g=2, i=tiles, u=2)
+            for n in groups[k]:
+                for tt in range(2):
+                    nc.scalar.copy(out=gf[:, :, 2 * (n - groups[k][0]) + tt],
+                                   in_=tbank[(n, tt)][:].rearrange("p (g u r) -> p g r u", g=2, u=2))
+            grp[k] = g
 
-        def quant(n):
-            c = cpool.tile([P, 512], U32, tag="codes", name="codes%d" % n, align_bytes=64)
-            s = cpool.tile([P, 512], U8, tag="scl", name="scl%d" % n, align_bytes=64)
-            nc.vector.quantize_mx(out=c[:].bitcast(FP8X4), scales=s[:], in_=grp[n][:])
-            codes[n] = (c, s)
+        def quant(k):
+            tiles = 2 * len(groups[k])
+            c = cpool.tile([P, tiles * 256], U32, tag="codes", name="codes%d" % k, align_bytes=64)
+            s = cpool.tile([P, tiles * 256], U8, tag="scl", name="scl%d" % k, align_bytes=64)
+            nc.vector.quantize_mx(out=c[:].bitcast(FP8X4), scales=s[:], in_=grp[k][:])
+            codes[k] = (c, s)
 
-        def mx(n):
-            c, s = codes[n]
-            xb = psum.tile([P, 2, 256], F32, tag="X%d" % (n % 2), name="X_%d" % n)
-            for tt in range(2):
+        def mx(k):
+            c, s = codes[k]
+            ntok = 256 * len(groups[k])
+            for f in range(2):
+                fb = psum.tile([P, ntok], F32, tag="F%d" % f, name="F%d_%d" % (f, k))
                 for g in range(2):
-                    lo = (2 * tt + g) * 128
+                    lo = 256 * g + 128 * f
                     nc.tensor.matmul_mx(
-                        out=xb[:, tt, :],
-                        lhsT=c[:, lo:lo + 128].bitcast(FP8X4), lhsT_scale=s[:, lo:lo + 128],
-                        rhs=wc[:, 256 * g:256 * (g + 1)].bitcast(FP8X4), rhs_scale=ws[:, 256 * g:256 * (g + 1)],
+                        out=fb[:],
+                        lhsT=wc[:, lo:lo + 128].bitcast(FP8X4), lhsT_scale=ws[:, lo:lo + 128],
+                        rhs=c[:, ntok * g:ntok * (g + 1)].bitcast(FP8X4), rhs_scale=s[:, ntok * g:ntok * (g + 1)],
                         start=(g == 0), stop=(g == 1))
-            xbank[n] = xb
+                fbank[(k, f)] = fb
 
-        def rbmm(n):
-            if a1_on_gpsimd(n) and n >= UPB:
-                return
-            t = 2 * (n % UPB)
-            rb = psum.tile([P, 2, 256], F32, tag="R%d" % (rcount[0] % 2), name="R_%d" % n)
-            rcount[0] += 1
+        def evac(k):
+            ntok = 256 * len(groups[k])
+            for f in range(2):
+                xt = epool.tile([P, ntok], F32, tag="xtb%d" % f, name="xtb%d_%d" % (f, k))
+                nc.scalar.activation(out=xt[:], in_=fbank[(k, f)][:], func=IDENT, bias=bcol[:, f:f + 1], scale=1.0)
+                xtb[(k, f)] = xt
+
+        def back(n):
+            k = group_index[n]
+            yb = psum.tile([P, 2, 256], F32, tag="Y%d" % (n % 2), name="Y_%d" % n)
             for tt in range(2):
-                nc.tensor.matmul(out=rb[:, tt, 0:192], lhsT=peT[:, t + tt, :], rhs=mb[:], start=True, stop=True)
-            if a1_on_gpsimd(n):
-                nc.scalar.copy(out=rbs[:, (n % UPB) // 2], in_=rb[:, :, 0:192])
-            else:
-                rbank[n] = rb
+                lo = 128 * (2 * (n - groups[k][0]) + tt)
+                for f in range(2):
+                    nc.tensor.transpose(yb[:, tt, 128 * f:128 * (f + 1)], xtb[(k, f)][:, lo:lo + 128], ident_f[:])
+            ybank[n] = yb
 
         def group_of(b, t):
             if b == NB - 1 and t >= 8:
                 return (8, 12) if t < 12 else (12, 16)
             return (0, 8) if t < 8 else (8, 16)
 
-        def rope_mul(n):
+        def rope(n):
             b = n // UPB
             t = 2 * (n % UPB)
             g0, g1 = group_of(b, t)
@@ -182,62 +186,22 @@ def tile_multiqueryattention_pa_t_kernel(tc, tensor, w_qkv, b_qkv, pos_emb, out_
                 ystage[b] = ypool.tile([P, 4, g1 - g0, 64], F32, tag="ys", name="ys%d_%d" % (b, g0))
             ys = ystage[b]
             tl = t - g0
-            xb = xbank[n]
-            m1 = mpool.tile([P, 2, 3, 64], F32, tag="m1", name="m1_%d" % n)
-            xr = xb[:, :, 0:192]
+            yb = ybank[n]
+            mu = mpool.tile([P, 2, 2, 3, 64], F32, tag="mu", name="mu_%d" % n)
             nc.vector.tensor_tensor(
-                out=m1[:], in0=xr.rearrange("p t (h d) -> p t h d", h=3),
-                in1=pe_sb[:, t:t + 2, 0:64].unsqueeze(2).to_broadcast([P, 2, 3, 64]), op=MULT)
-            xe = xr.rearrange("p t (h i e) -> p t h i e", h=3, e=2)
-            se = pe_sb[:, t:t + 2, 64:128].rearrange("p t (i e) -> p t i e", e=2)
-            if REV:
-                pl = mpool.tile([P, 2, 3, 64], F32, tag="pl", name="pl_%d" % n)
-                nc.vector.tensor_tensor(
-                    out=pl[:].rearrange("p t h (i e) -> p t h i e", e=2), in0=xe[:, :, :, :, ::-1],
-                    in1=se.unsqueeze(2).to_broadcast([P, 2, 3, 32, 2]), op=MULT)
+                out=mu[:],
+                in0=yb[:, :, 0:192].rearrange("p t (h d) -> p t h d", h=3).unsqueeze(2).to_broadcast([P, 2, 2, 3, 64]),
+                in1=tab[:, t:t + 2].unsqueeze(3).to_broadcast([P, 2, 2, 3, 64]), op=MULT)
+            if V_COPY_ON_VECTOR:
+                nc.vector.tensor_copy(out=ys[:, 3, tl:tl + 2, :], in_=yb[:, :, 192:256])
             else:
-                pl = mpool.tile([P, 2, 2, 3, 32], F32, tag="pl", name="pl_%d" % n)
-                for e in range(2):
-                    nc.vector.tensor_tensor(
-                        out=pl[:, e], in0=xe[:, :, :, :, 1 - e],
-                        in1=se[:, :, :, e].unsqueeze(2).to_broadcast([P, 2, 3, 32]), op=MULT)
-            if V_OFF_VECTOR:
-                nc.scalar.copy(out=ys[:, 3, tl:tl + 2, :], in_=xb[:, :, 192:256])
-            else:
-                nc.vector.tensor_tensor(
-                    out=ys[:, 3, tl:tl + 2, :], in0=xb[:, :, 192:256],
-                    in1=bb[:, 192:256].unsqueeze(1).to_broadcast([P, 2, 64]), op=ADD)
-            work[n] = (m1, pl)
-
-        def rope_add(n):
-            b = n // UPB
-            t = 2 * (n % UPB)
-            g0, g1 = group_of(b, t)
-            ys = ystage[b]
-            tl = t - g0
-            m1, pl = work[n]
-            if a1_on_gpsimd(n):
-                nc.gpsimd.tensor_tensor(
-                    out=m1[:], in0=m1[:],
-                    in1=rbs[:, (n % UPB) // 2].rearrange("p t (h d) -> p t h d", h=3), op=ADD)
-            else:
-                nc.vector.tensor_tensor(
-                    out=m1[:], in0=m1[:], in1=rbank[n][:, :, 0:192].rearrange("p t (h d) -> p t h d", h=3), op=ADD)
+                nc.scalar.copy(out=ys[:, 3, tl:tl + 2, :], in_=yb[:, :, 192:256])
             eng = nc.vector if (TAIL_ON_VECTOR and n == NU - 1) else nc.gpsimd
-            if REV:
-                eng.tensor_tensor(
-                    out=ys[:, 0:3, tl:tl + 2, :].rearrange("p h t d -> p t h d"),
-                    in0=m1[:], in1=pl[:], op=ADD)
-            else:
-                eng.tensor_tensor(
-                    out=ys[:, 0:3, tl:tl + 2, :].rearrange("p h t (i e) -> p t h i e", e=2),
-                    in0=m1[:].rearrange("p t h (i e) -> p t h i e", e=2),
-                    in1=pl[:].rearrange("p e t h i -> p t h i e"), op=ADD)
+            eng.tensor_tensor(
+                out=ys[:, 0:3, tl:tl + 2, :].rearrange("p h t (i e) -> p t h i e", e=2),
+                in0=mu[:, :, 0].rearrange("p t h (i e) -> p t h i e", e=2),
+                in1=mu[:, :, 1].rearrange("p t h (i e) -> p t h i e", e=2)[:, :, :, :, ::-1], op=ADD)
             if t + 2 == g1:
-                if V_OFF_VECTOR:
-                    nc.gpsimd.tensor_tensor(
-                        out=ys[:, 3, :, :], in0=ys[:, 3, :, :],
-                        in1=bb[:, 192:256].unsqueeze(1).to_broadcast([P, g1 - g0, 64]), op=ADD)
                 nc.sync.dma_start(out=out_0[b].rearrange("h (p t) d -> p h t d", t=TPP)[:, :, g0:g1, :],
                                   in_=ys[:, 0:2, :, :])
                 nc.sync.dma_start(out=out_1[b, 0].rearrange("(p t) d -> p t d", t=TPP)[:, g0:g1, :],
@@ -245,26 +209,27 @@ def tile_multiqueryattention_pa_t_kernel(tc, tensor, w_qkv, b_qkv, pos_emb, out_
                 nc.sync.dma_start(out=out_2[b, 0].rearrange("(p t) d -> p t d", t=TPP)[:, g0:g1, :],
                                   in_=ys[:, 3, :, :])
 
-        for s in range(-AHEAD, NU):
-            late = -1 <= s <= 0
-            if s + AHEAD < NU and not late:
-                transposes(s + AHEAD)
-                copies(s + AHEAD)
-            if 0 <= s + 1 < NU:
-                quant(s + 1)
-            if s >= 0:
-                rope_mul(s)
-            if 0 <= s + 1 < NU:
-                mx(s + 1)
-                if s == -1:
-                    for hf in range(2):
-                        tq = psum.tile([P, 8, 128], BF16, tag="R%d" % hf, name="tq%d" % hf)
-                        for j in range(8):
-                            nc.tensor.transpose(tq[:, j, :], pe_sb[:, 8 * hf + j, :], ident_b[:])
-                        nc.scalar.copy(out=peT[:, 8 * hf:8 * (hf + 1), :], in_=tq[:])
-                rbmm(s + 1)
-            if s >= 0:
-                rope_add(s)
-            if late:
-                transposes(s + AHEAD)
-                copies(s + AHEAD)
+        transposes(0)
+        copies(0)
+        transposes(1)
+        quant(0)
+        mx(0)
+        copies(1)
+        evac(0)
+        for k in range(NG):
+            if k >= 1 and k + 2 < NG:
+                copies(k + 2)
+            if k + 1 < NG:
+                quant(k + 1)
+            for n in groups[k]:
+                back(n)
+            for n in groups[k]:
+                rope(n)
+            if k + 1 < NG:
+                mx(k + 1)
+                evac(k + 1)
+            if k == 0:
+                transposes(2)
+                copies(2)
+            if k + 3 < NG:
+                transposes(k + 3)

@@ -24,6 +24,7 @@ NU = NB * UPB
 MANUAL = True
 V_COPY_ON_VECTOR = True
 TAIL_ON_VECTOR = True
+GATE = True
 
 
 def tile_multiqueryattention_pa_t_kernel(tc, tensor, w_qkv, b_qkv, pos_emb, out_0, out_1, out_2):
@@ -108,6 +109,8 @@ def tile_multiqueryattention_pa_t_kernel(tc, tensor, w_qkv, b_qkv, pos_emb, out_
         ws = const.tile([P, 512], U8, name="ws", align_bytes=64)
         nc.vector.quantize_mx(out=wc[:].bitcast(FP8X4), scales=ws[:], in_=wg[:])
 
+        gsc = const.tile([P, 1], F32, name="gsc") if GATE else None
+
         tbank = {}
         grp = {}
         codes = {}
@@ -142,6 +145,8 @@ def tile_multiqueryattention_pa_t_kernel(tc, tensor, w_qkv, b_qkv, pos_emb, out_
             s = cpool.tile([P, tiles * 256], U8, tag="scl", name="scl%d" % k, align_bytes=64)
             nc.vector.quantize_mx(out=c[:].bitcast(FP8X4), scales=s[:], in_=grp[k][:])
             codes[k] = (c, s)
+            if GATE:
+                nc.gpsimd.tensor_copy(out=gsc[:], in_=c[:, 0:1].bitcast(F32))
 
         def mx(k):
             c, s = codes[k]
@@ -178,7 +183,7 @@ def tile_multiqueryattention_pa_t_kernel(tc, tensor, w_qkv, b_qkv, pos_emb, out_
                 return (8, 12) if t < 12 else (12, 16)
             return (0, 8) if t < 8 else (8, 16)
 
-        def rope(n):
+        def rope_mul(n):
             b = n // UPB
             t = 2 * (n % UPB)
             g0, g1 = group_of(b, t)
@@ -196,6 +201,14 @@ def tile_multiqueryattention_pa_t_kernel(tc, tensor, w_qkv, b_qkv, pos_emb, out_
                 nc.vector.tensor_copy(out=ys[:, 3, tl:tl + 2, :], in_=yb[:, :, 192:256])
             else:
                 nc.scalar.copy(out=ys[:, 3, tl:tl + 2, :], in_=yb[:, :, 192:256])
+            work[n] = (mu, ys)
+
+        def rope_add(n):
+            b = n // UPB
+            t = 2 * (n % UPB)
+            g0, g1 = group_of(b, t)
+            tl = t - g0
+            mu, ys = work[n]
             eng = nc.vector if (TAIL_ON_VECTOR and n == NU - 1) else nc.gpsimd
             eng.tensor_tensor(
                 out=ys[:, 0:3, tl:tl + 2, :].rearrange("p h t (i e) -> p t h i e", e=2),
@@ -221,10 +234,14 @@ def tile_multiqueryattention_pa_t_kernel(tc, tensor, w_qkv, b_qkv, pos_emb, out_
                 copies(k + 2)
             if k + 1 < NG:
                 quant(k + 1)
+            if k >= 1:
+                rope_add(groups[k - 1][-1])
             for n in groups[k]:
                 back(n)
             for n in groups[k]:
-                rope(n)
+                rope_mul(n)
+                if n != groups[k][-1]:
+                    rope_add(n)
             if k + 1 < NG:
                 mx(k + 1)
                 evac(k + 1)
@@ -233,3 +250,4 @@ def tile_multiqueryattention_pa_t_kernel(tc, tensor, w_qkv, b_qkv, pos_emb, out_
                 copies(2)
             if k + 3 < NG:
                 transposes(k + 3)
+        rope_add(NU - 1)

@@ -35,7 +35,7 @@ def tile_multiqueryattention_pa_t_kernel(tc, tensor, w_qkv, b_qkv, pos_emb, out_
         gpool = ctx.enter_context(tc.tile_pool(name="gpool", bufs=2))
         cpool = ctx.enter_context(tc.tile_pool(name="cpool", bufs=2))
         epool = ctx.enter_context(tc.tile_pool(name="epool", bufs=2))
-        mpool = ctx.enter_context(tc.tile_pool(name="mpool", bufs=4))
+        mpool = ctx.enter_context(tc.tile_pool(name="mpool", bufs=5))
         ypool = ctx.enter_context(tc.tile_pool(name="ypool", bufs=3))
         psum = ctx.enter_context(tc.psum_pool(name="psum", bufs=1))
         if MANUAL:
@@ -145,8 +145,6 @@ def tile_multiqueryattention_pa_t_kernel(tc, tensor, w_qkv, b_qkv, pos_emb, out_
             s = cpool.tile([P, tiles * 256], U8, tag="scl", name="scl%d" % k, align_bytes=64)
             nc.vector.quantize_mx(out=c[:].bitcast(FP8X4), scales=s[:], in_=grp[k][:])
             codes[k] = (c, s)
-            if GATE:
-                nc.gpsimd.tensor_copy(out=gsc[:], in_=c[:, 0:1].bitcast(F32))
 
         def mx(k):
             c, s = codes[k]
@@ -203,17 +201,28 @@ def tile_multiqueryattention_pa_t_kernel(tc, tensor, w_qkv, b_qkv, pos_emb, out_
                 nc.scalar.copy(out=ys[:, 3, tl:tl + 2, :], in_=yb[:, :, 192:256])
             work[n] = (mu, ys)
 
-        def rope_add(n):
+        def rope_add(n, eng):
             b = n // UPB
             t = 2 * (n % UPB)
             g0, g1 = group_of(b, t)
             tl = t - g0
             mu, ys = work[n]
-            eng = nc.vector if (TAIL_ON_VECTOR and n == NU - 1) else nc.gpsimd
             eng.tensor_tensor(
                 out=ys[:, 0:3, tl:tl + 2, :].rearrange("p h t (i e) -> p t h i e", e=2),
                 in0=mu[:, :, 0].rearrange("p t h (i e) -> p t h i e", e=2),
                 in1=mu[:, :, 1].rearrange("p t h (i e) -> p t h i e", e=2)[:, :, :, :, ::-1], op=ADD)
+
+        def gate(n):
+            t = 2 * (n % UPB)
+            g0, g1 = group_of(n // UPB, t)
+            mu, ys = work[n]
+            nc.gpsimd.tensor_copy(out=gsc[:], in_=ys[:, 0, t - g0, 0:1])
+
+        def store(n):
+            b = n // UPB
+            t = 2 * (n % UPB)
+            g0, g1 = group_of(b, t)
+            mu, ys = work[n]
             if t + 2 == g1:
                 nc.sync.dma_start(out=out_0[b].rearrange("h (p t) d -> p h t d", t=TPP)[:, :, g0:g1, :],
                                   in_=ys[:, 0:2, :, :])
@@ -235,13 +244,18 @@ def tile_multiqueryattention_pa_t_kernel(tc, tensor, w_qkv, b_qkv, pos_emb, out_
             if k + 1 < NG:
                 quant(k + 1)
             if k >= 1:
-                rope_add(groups[k - 1][-1])
+                prev = groups[k - 1]
+                rope_add(prev[-1], nc.vector)
+                if len(prev) == 2:
+                    gate(prev[-1])
+                    rope_add(prev[0], nc.gpsimd)
+                store(prev[-1])
             for n in groups[k]:
                 back(n)
             for n in groups[k]:
                 rope_mul(n)
-                if n != groups[k][-1]:
-                    rope_add(n)
+                if k == NG - 1:
+                    rope_add(n, nc.gpsimd if n == groups[k][0] else nc.vector)
             if k + 1 < NG:
                 mx(k + 1)
                 evac(k + 1)
@@ -250,4 +264,4 @@ def tile_multiqueryattention_pa_t_kernel(tc, tensor, w_qkv, b_qkv, pos_emb, out_
                 copies(2)
             if k + 3 < NG:
                 transposes(k + 3)
-        rope_add(NU - 1)
+        store(NU - 1)

from contextlib import ExitStack

import concourse.mybir as mybir
from concourse.masks import make_identity

FLOPS = 2 * 8192 * 1024 * 256

F32 = mybir.dt.float32
BF16 = mybir.dt.bfloat16
U32 = mybir.dt.uint32
U8 = mybir.dt.uint8
FP8X4 = mybir.dt.float8_e4m3fn_x4
ADD = mybir.AluOpType.add
MULT = mybir.AluOpType.mult
IDENT = mybir.ActivationFunctionType.Identity

P = 128
NB = 4
TPP = 16
HID = 1024
UPB = TPP // 2
NU = NB * UPB

MANUAL = True
V_COPY_ON_VECTOR = True
TAIL_ON_VECTOR = True
GATE = True


def tile_multiqueryattention_pa_t_kernel(tc, tensor, w_qkv, b_qkv, pos_emb, out_0, out_1, out_2):
    nc = tc.nc
    with ExitStack() as ctx:
        const = ctx.enter_context(tc.tile_pool(name="const", bufs=1))
        xpool = ctx.enter_context(tc.tile_pool(name="xpool", bufs=1))
        gpool = ctx.enter_context(tc.tile_pool(name="gpool", bufs=2))
        cpool = ctx.enter_context(tc.tile_pool(name="cpool", bufs=2))
        epool = ctx.enter_context(tc.tile_pool(name="epool", bufs=2))
        mpool = ctx.enter_context(tc.tile_pool(name="mpool", bufs=5))
        ypool = ctx.enter_context(tc.tile_pool(name="ypool", bufs=3))
        psum = ctx.enter_context(tc.psum_pool(name="psum", bufs=1))
        if MANUAL:
            ctx.enter_context(tc.manual_schedule())

        groups = [[0], [1]] + [[n, n + 1] for n in range(2, NU, 2)]
        NG = len(groups)
        group_index = {}
        for k in range(NG):
            for n in groups[k]:
                group_index[n] = k

        bb = const.tile([P, 256], BF16, name="bb")
        nc.scalar.dma_start(out=bb[:], in_=b_qkv.partition_broadcast(P))
        w_sb = const.tile([P, 2, HID], BF16, name="w_sb")
        nc.sync.dma_start(out=w_sb[:], in_=w_qkv.rearrange("(a p) k -> p a k", p=P))
        xsrc = {}

        def load_x(n0, units):
            b = n0 // UPB
            t0 = 2 * (n0 % UPB)
            view = tensor[b].rearrange("(p t) k -> p t k", t=TPP)
            xt = xpool.tile([P, 2 * units, HID], BF16, name="x%d" % n0)
            nc.sync.dma_start(out=xt[:], in_=view[:, t0:t0 + 2 * units, :])
            for j in range(2 * units):
                xsrc[(n0 + j // 2, j % 2)] = xt[:, j, :]

        load_x(0, 1)
        load_x(1, 1)
        pe_sb = const.tile([P, TPP, 128], BF16, name="pe_sb")
        nc.sync.dma_start(out=pe_sb[:], in_=pos_emb.rearrange("(p t) c -> p t c", t=TPP))
        for n0 in range(2, NU, 2):
            load_x(n0, 2)

        ident_f = const.tile([P, P], F32, name="ident_f")
        make_identity(nc, ident_f[:])

        bsel = const.tile([P, 2, P], F32, name="bsel")
        nc.vector.tensor_tensor(
            out=bsel[:], in0=bb[:].rearrange("p (f j) -> p f j", f=2),
            in1=ident_f[:].unsqueeze(1).to_broadcast([P, 2, P]), op=MULT)
        bcol = const.tile([P, 2], F32, name="bcol")
        nc.vector.tensor_reduce(out=bcol[:], in_=bsel[:], axis=mybir.AxisListType.X, op=ADD)

        tab = const.tile([P, TPP, 2, 64], BF16, name="tab")

        def build_tab(ta0, ta1):
            cos_src = pe_sb[:, ta0:ta1, 0:64]
            sin_src = pe_sb[:, ta0:ta1, 64:128].rearrange("p t (i e) -> p t i e", e=2)[:, :, :, ::-1]
            sin_dst = tab[:, ta0:ta1, 1, :].rearrange("p t (i e) -> p t i e", e=2)
            nc.gpsimd.tensor_scalar(out=tab[:, ta0:ta1, 0, :], in0=cos_src, scalar1=1.0, scalar2=0.0,
                                    op0=MULT, op1=ADD)
            nc.gpsimd.tensor_scalar(out=sin_dst, in0=sin_src, scalar1=1.0, scalar2=0.0, op0=MULT, op1=ADD)

        build_tab(0, 4)
        build_tab(4, TPP)

        wg = const.tile([P, 2048], BF16, name="wg", align_bytes=64)
        wg_f = wg[:].bitcast(F32).rearrange("p (g n u) -> p g n u", g=2, u=2)
        for a in range(2):
            tw = psum.tile([P, 512], F32, tag="T%d" % (2 + a), name="tw%d" % a)
            wa = w_sb[:, a, :].bitcast(F32)
            for q in range(4):
                nc.tensor.transpose(tw[:, 128 * q:128 * (q + 1)], wa[:, 128 * q:128 * (q + 1)], ident_f[:])
            src = tw[:].rearrange("p (g u n) -> p g n u", g=2, u=2)
            if a == 0:
                nc.scalar.copy(out=wg_f[:, :, 0:128, :], in_=src)
            else:
                nc.vector.tensor_copy(out=wg_f[:, :, 128:256, :], in_=src)
        wc = const.tile([P, 512], U32, name="wc", align_bytes=64)
        ws = const.tile([P, 512], U8, name="ws", align_bytes=64)
        nc.vector.quantize_mx(out=wc[:].bitcast(FP8X4), scales=ws[:], in_=wg[:])

        gsc = const.tile([P, 1], F32, name="gsc") if GATE else None

        tbank = {}
        grp = {}
        codes = {}
        fbank = {}
        xtb = {}
        ybank = {}
        work = {}
        ystage = {}

        def transposes(k):
            for n in groups[k]:
                for tt in range(2):
                    tp = psum.tile([P, 512], F32, tag="T%d" % ((2 * n + tt) % 4), name="T%d_%d" % (tt, n))
                    xa = xsrc[(n, tt)].bitcast(F32)
                    for q in range(4):
                        nc.tensor.transpose(tp[:, 128 * q:128 * (q + 1)], xa[:, 128 * q:128 * (q + 1)], ident_f[:])
                    tbank[(n, tt)] = tp

        def copies(k):
            tiles = 2 * len(groups[k])
            g = gpool.tile([P, tiles * HID], BF16, tag="grp", name="grp%d" % k, align_bytes=64)
            gf = g[:].bitcast(F32).rearrange("p (g i r u) -> p g i r u", g=2, i=tiles, u=2)
            for n in groups[k]:
                for tt in range(2):
                    nc.scalar.copy(out=gf[:, :, 2 * (n - groups[k][0]) + tt],
                                   in_=tbank[(n, tt)][:].rearrange("p (g u r) -> p g r u", g=2, u=2))
            grp[k] = g

        def quant(k):
            tiles = 2 * len(groups[k])
            c = cpool.tile([P, tiles * 256], U32, tag="codes", name="codes%d" % k, align_bytes=64)
            s = cpool.tile([P, tiles * 256], U8, tag="scl", name="scl%d" % k, align_bytes=64)
            nc.vector.quantize_mx(out=c[:].bitcast(FP8X4), scales=s[:], in_=grp[k][:])
            codes[k] = (c, s)

        def mx(k):
            c, s = codes[k]
            ntok = 256 * len(groups[k])
            for f in range(2):
                fb = psum.tile([P, ntok], F32, tag="F%d" % f, name="F%d_%d" % (f, k))
                for g in range(2):
                    lo = 256 * g + 128 * f
                    nc.tensor.matmul_mx(
                        out=fb[:],
                        lhsT=wc[:, lo:lo + 128].bitcast(FP8X4), lhsT_scale=ws[:, lo:lo + 128],
                        rhs=c[:, ntok * g:ntok * (g + 1)].bitcast(FP8X4), rhs_scale=s[:, ntok * g:ntok * (g + 1)],
                        start=(g == 0), stop=(g == 1))
                fbank[(k, f)] = fb

        def evac(k):
            ntok = 256 * len(groups[k])
            for f in range(2):
                xt = epool.tile([P, ntok], F32, tag="xtb%d" % f, name="xtb%d_%d" % (f, k))
                nc.scalar.activation(out=xt[:], in_=fbank[(k, f)][:], func=IDENT, bias=bcol[:, f:f + 1], scale=1.0)
                xtb[(k, f)] = xt

        def back(n):
            k = group_index[n]
            yb = psum.tile([P, 2, 256], F32, tag="Y%d" % (n % 2), name="Y_%d" % n)
            for tt in range(2):
                lo = 128 * (2 * (n - groups[k][0]) + tt)
                for f in range(2):
                    nc.tensor.transpose(yb[:, tt, 128 * f:128 * (f + 1)], xtb[(k, f)][:, lo:lo + 128], ident_f[:])
            ybank[n] = yb

        def group_of(b, t):
            if b == NB - 1 and t >= 8:
                return (8, 12) if t < 12 else (12, 16)
            return (0, 8) if t < 8 else (8, 16)

        def rope_mul(n):
            b = n // UPB
            t = 2 * (n % UPB)
            g0, g1 = group_of(b, t)
            if t == g0:
                ystage[b] = ypool.tile([P, 4, g1 - g0, 64], F32, tag="ys", name="ys%d_%d" % (b, g0))
            ys = ystage[b]
            tl = t - g0
            yb = ybank[n]
            mu = mpool.tile([P, 2, 2, 3, 64], F32, tag="mu", name="mu_%d" % n)
            nc.vector.tensor_tensor(
                out=mu[:],
                in0=yb[:, :, 0:192].rearrange("p t (h d) -> p t h d", h=3).unsqueeze(2).to_broadcast([P, 2, 2, 3, 64]),
                in1=tab[:, t:t + 2].unsqueeze(3).to_broadcast([P, 2, 2, 3, 64]), op=MULT)
            if V_COPY_ON_VECTOR:
                nc.vector.tensor_copy(out=ys[:, 3, tl:tl + 2, :], in_=yb[:, :, 192:256])
            else:
                nc.scalar.copy(out=ys[:, 3, tl:tl + 2, :], in_=yb[:, :, 192:256])
            work[n] = (mu, ys)

        def rope_add(n, eng):
            b = n // UPB
            t = 2 * (n % UPB)
            g0, g1 = group_of(b, t)
            tl = t - g0
            mu, ys = work[n]
            eng.tensor_tensor(
                out=ys[:, 0:3, tl:tl + 2, :].rearrange("p h t (i e) -> p t h i e", e=2),
                in0=mu[:, :, 0].rearrange("p t h (i e) -> p t h i e", e=2),
                in1=mu[:, :, 1].rearrange("p t h (i e) -> p t h i e", e=2)[:, :, :, :, ::-1], op=ADD)

        def gate(n):
            t = 2 * (n % UPB)
            g0, g1 = group_of(n // UPB, t)
            mu, ys = work[n]
            nc.gpsimd.tensor_copy(out=gsc[:], in_=ys[:, 0, t - g0, 0:1])

        def store(n):
            b = n // UPB
            t = 2 * (n % UPB)
            g0, g1 = group_of(b, t)
            mu, ys = work[n]
            if t + 2 == g1:
                nc.sync.dma_start(out=out_0[b].rearrange("h (p t) d -> p h t d", t=TPP)[:, :, g0:g1, :],
                                  in_=ys[:, 0:2, :, :])
                nc.sync.dma_start(out=out_1[b, 0].rearrange("(p t) d -> p t d", t=TPP)[:, g0:g1, :],
                                  in_=ys[:, 2, :, :])
                nc.sync.dma_start(out=out_2[b, 0].rearrange("(p t) d -> p t d", t=TPP)[:, g0:g1, :],
                                  in_=ys[:, 3, :, :])

        transposes(0)
        copies(0)
        transposes(1)
        quant(0)
        mx(0)
        copies(1)
        evac(0)
        for k in range(NG):
            if k >= 1 and k + 2 < NG:
                copies(k + 2)
            if k + 1 < NG:
                quant(k + 1)
            if k >= 1:
                prev = groups[k - 1]
                rope_add(prev[-1], nc.vector)
                if len(prev) == 2:
                    gate(prev[-1])
                    rope_add(prev[0], nc.gpsimd)
                store(prev[-1])
            for n in groups[k]:
                back(n)
            for n in groups[k]:
                rope_mul(n)
                if k == NG - 1:
                    rope_add(n, nc.gpsimd if n == groups[k][0] else nc.vector)
            if k + 1 < NG:
                mx(k + 1)
                evac(k + 1)
            if k == 0:
                transposes(2)
                copies(2)
            if k + 3 < NG:
                transposes(k + 3)
        store(NU - 1)
